import numpy as np
import ml_dtypes


def mxq(x, axis, fmt="e4m3"):
    dtype, down = {"e4m3": (ml_dtypes.float8_e4m3fn, 7), "e5m2": (ml_dtypes.float8_e5m2, 14)}[fmt]
    v = np.moveaxis(np.asarray(x, np.float32).astype(ml_dtypes.bfloat16).astype(np.float64), axis, -1)
    blocks = v.reshape(v.shape[:-1] + (-1, 32))
    amax = np.abs(blocks).max(-1, keepdims=True)
    byte = np.maximum(np.where(amax > 0, np.frexp(amax)[1] - 1 + 127, 0) - down, 1)
    scale = np.exp2(byte - 127.0)
    codes = (blocks / scale).astype(np.float32).astype(dtype).astype(np.float64)
    return np.moveaxis((codes * scale).reshape(v.shape), -1, axis)


WIDE = False


def mx_kscale(k):
    if not WIDE:
        return np.ones(k)
    levels = np.array([10, -10, 5, -5, 0])
    a = np.random.permutation(np.resize(levels, k // 512 * 4)).reshape(k // 512, 4)
    idx = np.arange(k)
    return np.exp2(a[idx // 512, idx % 128 // 32])


BF16 = ml_dtypes.bfloat16


def bf(x):
    return np.asarray(x, np.float32).astype(BF16)


def f64(x):
    return np.asarray(x).astype(np.float64)


E2M1 = np.array([0.0, 0.5, 1.0, 1.5, 2.0, 3.0, 4.0, 6.0, -0.0, -0.5, -1.0, -1.5, -2.0, -3.0, -4.0, -6.0])


def pack_weight(w, fmt):
    k, n = w.shape
    w = f64(bf(w)).reshape(k // 32, 32, n)
    amax = np.abs(w).max(1)
    if fmt == "e4m3":
        byte = np.frexp(amax)[1] - 1 + 127 - 7
    else:
        mant, ex = np.frexp(amax / 6.0)
        byte = np.where(mant > 0.5, ex, ex - 1) + 127
    byte = np.clip(np.where(amax > 0, byte, 1), 1, 254)
    scaled = (w * np.exp2(127.0 - byte)[:, None, :]).reshape(k, n).astype(np.float32)
    by_word = np.ascontiguousarray(scaled.reshape(k // 512, 128, 4, n).transpose(0, 1, 3, 2))
    if fmt == "e4m3":
        words = by_word.astype(ml_dtypes.float8_e4m3fn).view(np.uint8)
    else:
        c = by_word.astype(ml_dtypes.float4_e2m1fn).view(np.uint8) & 0xF
        words = c[..., 0::2] | (c[..., 1::2] << 4)
    return np.ascontiguousarray(words), np.ascontiguousarray(byte.astype(np.uint8).reshape(k // 512, 16, n))


def unpack_weight(words, scales, fmt):
    g, p, n, _ = words.shape
    if fmt == "e4m3":
        vals = np.ascontiguousarray(words).view(ml_dtypes.float8_e4m3fn).astype(np.float64)
    else:
        nib = np.empty((g, p, n, 4), np.uint8)
        nib[..., 0::2] = words & 0xF
        nib[..., 1::2] = words >> 4
        vals = E2M1[nib]
    vals = vals * np.repeat(np.exp2(scales.astype(np.float64) - 127.0), 8, axis=1)[..., None]
    return vals.transpose(0, 1, 3, 2).reshape(g * 512, n)


I, H, B = 2048, 2048, 128
FMT = "e4m3"


def sigmoid(v):
    return 1.0 / (1.0 + np.exp(-v))


def setup_inputs():
    s, t = mx_kscale(I), mx_kscale(H)
    d = {"x": bf(np.random.standard_normal((I, B)) * s[:, None]), "h": bf(np.random.standard_normal((B, H)) * t[None, :])}
    for n in ("w_ii", "w_ig"):
        w = np.random.standard_normal((H, I)) * 0.7 / np.sqrt(I) / s[None, :]
        d[n + "_words"], d[n + "_scales"] = pack_weight(np.ascontiguousarray(w.T), FMT)
    for n in ("w_hi", "w_hg"):
        w = np.random.standard_normal((H, H)) * 0.7 / np.sqrt(H) / t[None, :]
        d[n + "_words"], d[n + "_scales"] = pack_weight(np.ascontiguousarray(w.T), FMT)
    for n in ("b_ii", "b_hi", "b_ig", "b_hg"):
        d[n] = bf(np.random.standard_normal((H, 1)) * 0.3)
    return d


def reference(x, h, w_ii_words, w_ii_scales, w_ig_words, w_ig_scales, w_hi_words, w_hi_scales, w_hg_words, w_hg_scales, b_ii, b_hi, b_ig, b_hg):
    xq = mxq(f64(x), 0, "e4m3")
    hq = mxq(f64(h).T, 0, "e4m3")
    i = sigmoid((unpack_weight(w_ii_words, w_ii_scales, FMT).T @ xq) + f64(b_ii) + (unpack_weight(w_hi_words, w_hi_scales, FMT).T @ hq) + f64(b_hi))
    g = np.tanh((unpack_weight(w_ig_words, w_ig_scales, FMT).T @ xq) + f64(b_ig) + (unpack_weight(w_hg_words, w_hg_scales, FMT).T @ hq) + f64(b_hg))
    return i * g

@@ -1,0 +1,207 @@
+from contextlib import ExitStack
+
+import concourse.mybir as mybir
+from concourse.masks import make_identity
+
+F32 = mybir.dt.float32
+BF16 = mybir.dt.bfloat16
+I32 = mybir.dt.int32
+U32 = mybir.dt.uint32
+U8 = mybir.dt.uint8
+FP8X4 = mybir.dt.float8_e4m3fn_x4
+ACT = mybir.ActivationFunctionType
+
+P = 128
+PACK = 4
+K = 2048
+GROUPS = K // (P * PACK)
+HIDDEN = 2048
+BATCH = 128
+HALVES = 2
+HALF = HIDDEN // HALVES
+TILES = HALF // P
+QUADS = 4
+LIVE = 16
+STORE_TILES = 4
+
+FLOPS = 2 * 4 * HIDDEN * K * BATCH
+
+
+def tile_naivelstm_pa_kernel(
+    tc,
+    x,
+    h,
+    w_ii_words,
+    w_ii_scales,
+    w_ig_words,
+    w_ig_scales,
+    w_hi_words,
+    w_hi_scales,
+    w_hg_words,
+    w_hg_scales,
+    b_ii,
+    b_hi,
+    b_ig,
+    b_hg,
+    out,
+):
+    nc = tc.nc
+    words = {"ii": w_ii_words, "hi": w_hi_words, "ig": w_ig_words, "hg": w_hg_words}
+    scales = {"ii": w_ii_scales, "hi": w_hi_scales, "ig": w_ig_scales, "hg": w_hg_scales}
+    gate_weights = {"i": ("ii", "hi"), "g": ("ig", "hg")}
+    gate_column = {"i": 0, "g": 1}
+    phases = [(half, gate) for half in range(HALVES) for gate in ("i", "g")]
+
+    with ExitStack() as ctx:
+        ctx.enter_context(tc.manual_schedule())
+        keep = ctx.enter_context(tc.tile_pool(name="keep", bufs=1))
+
+        x_rows = keep.tile([P, GROUPS, PACK * BATCH], BF16)
+        h_rows = keep.tile([P, K], BF16)
+        bias_rows = keep.tile([P, P], BF16)
+        planes = {}
+        for w in ("ii", "hi", "ig", "hg"):
+            planes[w] = keep.tile([P, HIDDEN], U8, name="planes_" + w, align_bytes=64)
+        chunks = {}
+        for half, gate in phases:
+            for w in gate_weights[gate]:
+                for g in range(GROUPS):
+                    chunks[(half, w, g)] = keep.tile(
+                        [P, HALF], U32, name="chunk_%d_%s_%d" % (half, w, g), align_bytes=64
+                    )
+
+        for w in ("ii", "hi", "ig", "hg"):
+            nc.vector.memset(planes[w][:].bitcast(I32), 0)
+        nc.vector.memset(bias_rows[:], 0.0)
+
+        nc.sync.dma_start(
+            out=x_rows[:], in_=x.rearrange("(g p t) b -> p g (t b)", p=P, t=PACK)
+        )
+        nc.sync.dma_start(out=h_rows[:], in_=h)
+        for i, b in enumerate((b_ii, b_hi, b_ig, b_hg)):
+            rows = HIDDEN // P
+            nc.scalar.dma_start(
+                out=bias_rows[rows * i : rows * (i + 1), :],
+                in_=b.rearrange("(j p) o -> j (p o)", p=P),
+            )
+        for w in ("ii", "hi", "ig", "hg"):
+            for quad in range(QUADS):
+                nc.sync.dma_start(
+                    out=planes[w][32 * quad : 32 * quad + LIVE, :].bitcast(I32),
+                    in_=scales[w][:, 4 * quad : 4 * quad + 4, :].bitcast(I32),
+                )
+        for half, gate in phases:
+            for w in gate_weights[gate]:
+                for g in range(GROUPS):
+                    half_bytes = slice(PACK * HALF * half, PACK * HALF * (half + 1))
+                    nc.sync.dma_start(
+                        out=chunks[(half, w, g)][:].bitcast(I32),
+                        in_=words[w][g].rearrange("p n t -> p (n t)")[:, half_bytes].bitcast(I32),
+                    )
+
+        x_grouped = keep.tile([P, GROUPS, BATCH, PACK], BF16, align_bytes=64)
+        nc.vector.tensor_copy(
+            out=x_grouped[:], in_=x_rows[:].rearrange("p g (t b) -> p g b t", t=PACK)
+        )
+        x_codes = keep.tile([P, GROUPS * BATCH], U32, align_bytes=64)
+        x_plane = keep.tile([P, GROUPS * BATCH], U8, align_bytes=64)
+
+        ident_f32 = keep.tile([P, P], F32)
+        make_identity(nc, ident_f32[:])
+        ident_bf16 = keep.tile([P, P], BF16)
+        make_identity(nc, ident_bf16[:])
+        h_grouped = keep.tile([P, GROUPS, BATCH, PACK], BF16, align_bytes=64)
+        h_codes = keep.tile([P, GROUPS * BATCH], U32, align_bytes=64)
+        h_plane = keep.tile([P, GROUPS * BATCH], U8, align_bytes=64)
+        bias_f32 = keep.tile([P, 2, 2, HIDDEN // P], F32)
+        bias_sum = keep.tile([P, 2, HIDDEN // P], F32)
+        with tc.psum_pool(name="turn", bufs=1) as turn:
+            h_words = h_rows[:].bitcast(F32)
+            h_grouped_words = (
+                h_grouped[:]
+                .rearrange("p g b t -> p (g b t)")
+                .bitcast(F32)
+                .rearrange("p (g b u) -> p g b u", g=GROUPS, u=2)
+            )
+            for pair in range(GROUPS // 2):
+                turned = turn.tile([P, 2, 2, BATCH], F32, name="turned_%d" % pair)
+                for gg in range(2):
+                    g = 2 * pair + gg
+                    for u in range(2):
+                        nc.tensor.transpose(
+                            turned[:, gg, u, :],
+                            h_words[:, 256 * g + u : 256 * (g + 1) : 2],
+                            ident_f32[:],
+                        )
+                nc.vector.tensor_copy(
+                    out=h_grouped_words[:, 2 * pair : 2 * pair + 2, :, :],
+                    in_=turned[:].rearrange("p g u b -> p g b u"),
+                )
+            nc.vector.quantize_mx(
+                out=x_codes[:].bitcast(FP8X4),
+                scales=x_plane[:],
+                in_=x_grouped[:].rearrange("p g b t -> p (g b t)"),
+            )
+            nc.vector.quantize_mx(
+                out=h_codes[:].bitcast(FP8X4),
+                scales=h_plane[:],
+                in_=h_grouped[:].rearrange("p g b t -> p (g b t)"),
+            )
+            bias_cols = turn.tile([P, P], BF16)
+            nc.tensor.transpose(bias_cols[:], bias_rows[:], ident_bf16[:])
+            nc.vector.tensor_copy(
+                out=bias_f32[:].rearrange("p a s j -> p (a s j)"), in_=bias_cols[:, 0 : P // 2]
+            )
+            nc.vector.tensor_add(
+                out=bias_sum[:], in0=bias_f32[:, :, 0, :], in1=bias_f32[:, :, 1, :]
+            )
+        moving = {"ii": (x_codes, x_plane), "ig": (x_codes, x_plane)}
+        moving["hi"] = (h_codes, h_plane)
+        moving["hg"] = (h_codes, h_plane)
+
+        psum = ctx.enter_context(tc.psum_pool(name="psum", bufs=1))
+        gate_i = keep.tile([P, HALVES * TILES, BATCH], F32)
+        gate_g = keep.tile([P, HALVES * TILES, BATCH], F32)
+        product = keep.tile([P, HALVES * TILES, BATCH], F32)
+        out_tiles = out.rearrange("(j p) b -> p j b", p=P)
+        for half, gate in phases:
+            sums = []
+            for j in range(TILES):
+                sums.append(psum.tile([P, BATCH], F32, name="sum_%d" % j, tag="sum_%d" % j))
+            for w in gate_weights[gate]:
+                codes, plane = moving[w]
+                for g in range(GROUPS):
+                    first = w == gate_weights[gate][0] and g == 0
+                    last = w == gate_weights[gate][1] and g == GROUPS - 1
+                    batch_cols = slice(BATCH * g, BATCH * (g + 1))
+                    for j in range(TILES):
+                        nc.tensor.matmul_mx(
+                            out=sums[j][:],
+                            lhsT=chunks[(half, w, g)][:, P * j : P * (j + 1)].bitcast(FP8X4),
+                            lhsT_scale=planes[w][
+                                4 * g : P, HALF * half + P * j : HALF * half + P * (j + 1)
+                            ],
+                            rhs=codes[:, batch_cols].bitcast(FP8X4),
+                            rhs_scale=plane[:, batch_cols],
+                            start=first,
+                            stop=last,
+                        )
+            for j in range(TILES):
+                tile_index = TILES * half + j
+                bias = bias_sum[:, gate_column[gate], tile_index : tile_index + 1]
+                if gate == "i":
+                    nc.scalar.activation(
+                        out=gate_i[:, tile_index, :], in_=sums[j][:], func=ACT.Sigmoid, bias=bias
+                    )
+                else:
+                    nc.scalar.activation(
+                        out=gate_g[:, tile_index, :], in_=sums[j][:], func=ACT.Tanh, bias=bias
+                    )
+                    nc.vector.tensor_mul(
+                        out=product[:, tile_index, :],
+                        in0=gate_i[:, tile_index, :],
+                        in1=gate_g[:, tile_index, :],
+                    )
+                    if (j + 1) % STORE_TILES == 0:
+                        done = slice(tile_index + 1 - STORE_TILES, tile_index + 1)
+                        nc.sync.dma_start(out=out_tiles[:, done, :], in_=product[:, done, :])

@@ -74,6 +74,11 @@ def tile_naivelstm_pa_kernel(
             nc.vector.memset(planes[w][:].bitcast(I32), 0)
         nc.vector.memset(bias_rows[:], 0.0)
 
+        ident_f32 = keep.tile([P, P], F32)
+        make_identity(nc, ident_f32[:])
+        ident_bf16 = keep.tile([P, P], BF16)
+        make_identity(nc, ident_bf16[:])
+
         nc.sync.dma_start(
             out=x_rows[:], in_=x.rearrange("(g p t) b -> p g (t b)", p=P, t=PACK)
         )
@@ -86,9 +91,9 @@ def tile_naivelstm_pa_kernel(
             )
         for w in ("ii", "hi", "ig", "hg"):
             for quad in range(QUADS):
-                nc.sync.dma_start(
-                    out=planes[w][32 * quad : 32 * quad + LIVE, :].bitcast(I32),
-                    in_=scales[w][:, 4 * quad : 4 * quad + 4, :].bitcast(I32),
+                nc.gpsimd.dma_start(
+                    out=planes[w][32 * quad : 32 * quad + LIVE, :].bitcast(F32),
+                    in_=scales[w][:, 4 * quad : 4 * quad + 4, :].bitcast(F32),
                 )
         for half, gate in phases:
             for w in gate_weights[gate]:
@@ -106,10 +111,6 @@ def tile_naivelstm_pa_kernel(
         x_codes = keep.tile([P, GROUPS * BATCH], U32, align_bytes=64)
         x_plane = keep.tile([P, GROUPS * BATCH], U8, align_bytes=64)
 
-        ident_f32 = keep.tile([P, P], F32)
-        make_identity(nc, ident_f32[:])
-        ident_bf16 = keep.tile([P, P], BF16)
-        make_identity(nc, ident_bf16[:])
         h_grouped = keep.tile([P, GROUPS, BATCH, PACK], BF16, align_bytes=64)
         h_codes = keep.tile([P, GROUPS * BATCH], U32, align_bytes=64)
         h_plane = keep.tile([P, GROUPS * BATCH], U8, align_bytes=64)

@@ -50,7 +50,7 @@ def tile_naivelstm_pa_kernel(
     scales = {"ii": w_ii_scales, "hi": w_hi_scales, "ig": w_ig_scales, "hg": w_hg_scales}
     gate_weights = {"i": ("ii", "hi"), "g": ("ig", "hg")}
     gate_column = {"i": 0, "g": 1}
-    phases = [(half, gate) for half in range(HALVES) for gate in ("i", "g")]
+    phases = [(half, gate) for gate in ("i", "g") for half in range(HALVES)]
 
     with ExitStack() as ctx:
         ctx.enter_context(tc.manual_schedule())

@@ -22,7 +22,8 @@ HALF = HIDDEN // HALVES
 TILES = HALF // P
 QUADS = 4
 LIVE = 16
-STORE_TILES = 4
+STORE_TILES = 2
+LAST_CUTS = 2
 
 FLOPS = 2 * 4 * HIDDEN * K * BATCH
 
@@ -51,6 +52,16 @@ def tile_naivelstm_pa_kernel(
     gate_weights = {"i": ("ii", "hi"), "g": ("ig", "hg")}
     gate_column = {"i": 0, "g": 1}
     phases = [(half, gate) for gate in ("i", "g") for half in range(HALVES)]
+    phase_chunks = []
+    for half, gate in phases:
+        chunk_list = []
+        for w in gate_weights[gate]:
+            is_last_weight = (half, gate) == phases[-1] and w == gate_weights[gate][-1]
+            cuts = LAST_CUTS if is_last_weight else 1
+            for cut in range(cuts):
+                for g in range(GROUPS):
+                    chunk_list.append((w, g, cut * (TILES // cuts), TILES // cuts))
+        phase_chunks.append(chunk_list)
 
     with ExitStack() as ctx:
         ctx.enter_context(tc.manual_schedule())
@@ -62,13 +73,15 @@ def tile_naivelstm_pa_kernel(
         planes = {}
         for w in ("ii", "hi", "ig", "hg"):
             planes[w] = keep.tile([P, HIDDEN], U8, name="planes_" + w, align_bytes=64)
-        chunks = {}
-        for half, gate in phases:
-            for w in gate_weights[gate]:
-                for g in range(GROUPS):
-                    chunks[(half, w, g)] = keep.tile(
-                        [P, HALF], U32, name="chunk_%d_%s_%d" % (half, w, g), align_bytes=64
-                    )
+        chunk_words = {}
+        for (half, gate), chunk_list in zip(phases, phase_chunks):
+            for w, g, tile0, tiles in chunk_list:
+                chunk_words[(half, w, g, tile0)] = keep.tile(
+                    [P, P * tiles],
+                    U32,
+                    name="words_%d_%s_%d_%d" % (half, w, g, tile0),
+                    align_bytes=64,
+                )
 
         for w in ("ii", "hi", "ig", "hg"):
             nc.vector.memset(planes[w][:].bitcast(I32), 0)
@@ -95,14 +108,14 @@ def tile_naivelstm_pa_kernel(
                     out=planes[w][32 * quad : 32 * quad + LIVE, :].bitcast(F32),
                     in_=scales[w][:, 4 * quad : 4 * quad + 4, :].bitcast(F32),
                 )
-        for half, gate in phases:
-            for w in gate_weights[gate]:
-                for g in range(GROUPS):
-                    half_bytes = slice(PACK * HALF * half, PACK * HALF * (half + 1))
-                    nc.sync.dma_start(
-                        out=chunks[(half, w, g)][:].bitcast(I32),
-                        in_=words[w][g].rearrange("p n t -> p (n t)")[:, half_bytes].bitcast(I32),
-                    )
+        for (half, gate), chunk_list in zip(phases, phase_chunks):
+            for w, g, tile0, tiles in chunk_list:
+                n0 = HALF * half + P * tile0
+                chunk_bytes = slice(PACK * n0, PACK * (n0 + P * tiles))
+                nc.sync.dma_start(
+                    out=chunk_words[(half, w, g, tile0)][:].bitcast(I32),
+                    in_=words[w][g].rearrange("p n t -> p (n t)")[:, chunk_bytes].bitcast(I32),
+                )
 
         x_grouped = keep.tile([P, GROUPS, BATCH, PACK], BF16, align_bytes=64)
         nc.vector.tensor_copy(
@@ -165,44 +178,48 @@ def tile_naivelstm_pa_kernel(
         gate_g = keep.tile([P, HALVES * TILES, BATCH], F32)
         product = keep.tile([P, HALVES * TILES, BATCH], F32)
         out_tiles = out.rearrange("(j p) b -> p j b", p=P)
-        for half, gate in phases:
+
+        def finish_tile(gate, tile_index, tile_sum):
+            bias = bias_sum[:, gate_column[gate], tile_index : tile_index + 1]
+            if gate == "i":
+                nc.scalar.activation(
+                    out=gate_i[:, tile_index, :], in_=tile_sum[:], func=ACT.Sigmoid, bias=bias
+                )
+            else:
+                nc.scalar.activation(
+                    out=gate_g[:, tile_index, :], in_=tile_sum[:], func=ACT.Tanh, bias=bias
+                )
+                nc.vector.tensor_mul(
+                    out=product[:, tile_index, :],
+                    in0=gate_i[:, tile_index, :],
+                    in1=gate_g[:, tile_index, :],
+                )
+                if (tile_index + 1) % STORE_TILES == 0:
+                    done = slice(tile_index + 1 - STORE_TILES, tile_index + 1)
+                    nc.sync.dma_start(out=out_tiles[:, done, :], in_=product[:, done, :])
+
+        for (half, gate), chunk_list in zip(phases, phase_chunks):
             sums = []
             for j in range(TILES):
                 sums.append(psum.tile([P, BATCH], F32, name="sum_%d" % j, tag="sum_%d" % j))
-            for w in gate_weights[gate]:
+            for w, g, tile0, tiles in chunk_list:
                 codes, plane = moving[w]
-                for g in range(GROUPS):
-                    first = w == gate_weights[gate][0] and g == 0
-                    last = w == gate_weights[gate][1] and g == GROUPS - 1
-                    batch_cols = slice(BATCH * g, BATCH * (g + 1))
-                    for j in range(TILES):
-                        nc.tensor.matmul_mx(
-                            out=sums[j][:],
-                            lhsT=chunks[(half, w, g)][:, P * j : P * (j + 1)].bitcast(FP8X4),
-                            lhsT_scale=planes[w][
-                                4 * g : P, HALF * half + P * j : HALF * half + P * (j + 1)
-                            ],
-                            rhs=codes[:, batch_cols].bitcast(FP8X4),
-                            rhs_scale=plane[:, batch_cols],
-                            start=first,
-                            stop=last,
-                        )
-            for j in range(TILES):
-                tile_index = TILES * half + j
-                bias = bias_sum[:, gate_column[gate], tile_index : tile_index + 1]
-                if gate == "i":
-                    nc.scalar.activation(
-                        out=gate_i[:, tile_index, :], in_=sums[j][:], func=ACT.Sigmoid, bias=bias
+                opens = w == gate_weights[gate][0] and g == 0
+                closes = w == gate_weights[gate][1] and g == GROUPS - 1
+                batch_cols = slice(BATCH * g, BATCH * (g + 1))
+                for j in range(tile0, tile0 + tiles):
+                    n0 = HALF * half + P * j
+                    nc.tensor.matmul_mx(
+                        out=sums[j][:],
+                        lhsT=chunk_words[(half, w, g, tile0)][
+                            :, P * (j - tile0) : P * (j - tile0 + 1)
+                        ].bitcast(FP8X4),
+                        lhsT_scale=planes[w][4 * g : P, n0 : n0 + P],
+                        rhs=codes[:, batch_cols].bitcast(FP8X4),
+                        rhs_scale=plane[:, batch_cols],
+                        start=opens,
+                        stop=closes,
                     )
-                else:
-                    nc.scalar.activation(
-                        out=gate_g[:, tile_index, :], in_=sums[j][:], func=ACT.Tanh, bias=bias
-                    )
-                    nc.vector.tensor_mul(
-                        out=product[:, tile_index, :],
-                        in0=gate_i[:, tile_index, :],
-                        in1=gate_g[:, tile_index, :],
-                    )
-                    if (j + 1) % STORE_TILES == 0:
-                        done = slice(tile_index + 1 - STORE_TILES, tile_index + 1)
-                        nc.sync.dma_start(out=out_tiles[:, done, :], in_=product[:, done, :])
+                if closes:
+                    for j in range(tile0, tile0 + tiles):
+                        finish_tile(gate, TILES * half + j, sums[j])

@@ -24,6 +24,8 @@ QUADS = 4
 LIVE = 16
 STORE_TILES = 2
 LAST_CUTS = 2
+LAST_PIECES = (2, 1, 1)
+SINGLE_STORES = 2
 
 FLOPS = 2 * 4 * HIDDEN * K * BATCH
 
@@ -60,7 +62,13 @@ def tile_naivelstm_pa_kernel(
             cuts = LAST_CUTS if is_last_weight else 1
             for cut in range(cuts):
                 for g in range(GROUPS):
-                    chunk_list.append((w, g, cut * (TILES // cuts), TILES // cuts))
+                    if is_last_weight and cut == cuts - 1 and g == GROUPS - 1:
+                        tile0 = TILES - sum(LAST_PIECES)
+                        for tiles in LAST_PIECES:
+                            chunk_list.append((w, g, tile0, tiles))
+                            tile0 += tiles
+                    else:
+                        chunk_list.append((w, g, cut * (TILES // cuts), TILES // cuts))
         phase_chunks.append(chunk_list)
 
     with ExitStack() as ctx:
@@ -74,6 +82,7 @@ def tile_naivelstm_pa_kernel(
         for w in ("ii", "hi", "ig", "hg"):
             planes[w] = keep.tile([P, HIDDEN], U8, name="planes_" + w, align_bytes=64)
         chunk_words = {}
+        words_of = {}
         for (half, gate), chunk_list in zip(phases, phase_chunks):
             for w, g, tile0, tiles in chunk_list:
                 chunk_words[(half, w, g, tile0)] = keep.tile(
@@ -82,6 +91,10 @@ def tile_naivelstm_pa_kernel(
                     name="words_%d_%s_%d_%d" % (half, w, g, tile0),
                     align_bytes=64,
                 )
+                for j in range(tiles):
+                    words_of[(half, w, g, tile0 + j)] = chunk_words[(half, w, g, tile0)][
+                        :, P * j : P * (j + 1)
+                    ]
 
         for w in ("ii", "hi", "ig", "hg"):
             nc.vector.memset(planes[w][:].bitcast(I32), 0)
@@ -194,8 +207,10 @@ def tile_naivelstm_pa_kernel(
                     in0=gate_i[:, tile_index, :],
                     in1=gate_g[:, tile_index, :],
                 )
-                if (tile_index + 1) % STORE_TILES == 0:
-                    done = slice(tile_index + 1 - STORE_TILES, tile_index + 1)
+                single = tile_index >= HALVES * TILES - SINGLE_STORES
+                if single or (tile_index + 1) % STORE_TILES == 0:
+                    first = tile_index if single else tile_index + 1 - STORE_TILES
+                    done = slice(first, tile_index + 1)
                     nc.sync.dma_start(out=out_tiles[:, done, :], in_=product[:, done, :])
 
         for (half, gate), chunk_list in zip(phases, phase_chunks):
@@ -211,9 +226,7 @@ def tile_naivelstm_pa_kernel(
                     n0 = HALF * half + P * j
                     nc.tensor.matmul_mx(
                         out=sums[j][:],
-                        lhsT=chunk_words[(half, w, g, tile0)][
-                            :, P * (j - tile0) : P * (j - tile0 + 1)
-                        ].bitcast(FP8X4),
+                        lhsT=words_of[(half, w, g, j)].bitcast(FP8X4),
                         lhsT_scale=planes[w][4 * g : P, n0 : n0 + P],
                         rhs=codes[:, batch_cols].bitcast(FP8X4),
                         rhs_scale=plane[:, batch_cols],

@@ -70,6 +70,10 @@ def tile_naivelstm_pa_kernel(
                     else:
                         chunk_list.append((w, g, cut * (TILES // cuts), TILES // cuts))
         phase_chunks.append(chunk_list)
+    loads = [(w, g, 0, HALVES * TILES) for w in gate_weights["i"] for g in range(GROUPS)]
+    for (half, gate), chunk_list in zip(phases, phase_chunks):
+        if gate == "g":
+            loads.extend((w, g, TILES * half + tile0, tiles) for w, g, tile0, tiles in chunk_list)
 
     with ExitStack() as ctx:
         ctx.enter_context(tc.manual_schedule())
@@ -81,20 +85,15 @@ def tile_naivelstm_pa_kernel(
         planes = {}
         for w in ("ii", "hi", "ig", "hg"):
             planes[w] = keep.tile([P, HIDDEN], U8, name="planes_" + w, align_bytes=64)
-        chunk_words = {}
+        load_tiles = []
         words_of = {}
-        for (half, gate), chunk_list in zip(phases, phase_chunks):
-            for w, g, tile0, tiles in chunk_list:
-                chunk_words[(half, w, g, tile0)] = keep.tile(
-                    [P, P * tiles],
-                    U32,
-                    name="words_%d_%s_%d_%d" % (half, w, g, tile0),
-                    align_bytes=64,
-                )
-                for j in range(tiles):
-                    words_of[(half, w, g, tile0 + j)] = chunk_words[(half, w, g, tile0)][
-                        :, P * j : P * (j + 1)
-                    ]
+        for w, g, first, tiles in loads:
+            load_tile = keep.tile(
+                [P, P * tiles], U32, name="words_%s_%d_%d" % (w, g, first), align_bytes=64
+            )
+            load_tiles.append(load_tile)
+            for j in range(tiles):
+                words_of[(w, g, first + j)] = load_tile[:, P * j : P * (j + 1)]
 
         for w in ("ii", "hi", "ig", "hg"):
             nc.vector.memset(planes[w][:].bitcast(I32), 0)
@@ -121,14 +120,12 @@ def tile_naivelstm_pa_kernel(
                     out=planes[w][32 * quad : 32 * quad + LIVE, :].bitcast(F32),
                     in_=scales[w][:, 4 * quad : 4 * quad + 4, :].bitcast(F32),
                 )
-        for (half, gate), chunk_list in zip(phases, phase_chunks):
-            for w, g, tile0, tiles in chunk_list:
-                n0 = HALF * half + P * tile0
-                chunk_bytes = slice(PACK * n0, PACK * (n0 + P * tiles))
-                nc.sync.dma_start(
-                    out=chunk_words[(half, w, g, tile0)][:].bitcast(I32),
-                    in_=words[w][g].rearrange("p n t -> p (n t)")[:, chunk_bytes].bitcast(I32),
-                )
+        for (w, g, first, tiles), load_tile in zip(loads, load_tiles):
+            load_bytes = slice(PACK * P * first, PACK * P * (first + tiles))
+            nc.sync.dma_start(
+                out=load_tile[:].bitcast(I32),
+                in_=words[w][g].rearrange("p n t -> p (n t)")[:, load_bytes].bitcast(I32),
+            )
 
         x_grouped = keep.tile([P, GROUPS, BATCH, PACK], BF16, align_bytes=64)
         nc.vector.tensor_copy(
@@ -226,7 +223,7 @@ def tile_naivelstm_pa_kernel(
                     n0 = HALF * half + P * j
                     nc.tensor.matmul_mx(
                         out=sums[j][:],
-                        lhsT=words_of[(half, w, g, j)].bitcast(FP8X4),
+                        lhsT=words_of[(w, g, TILES * half + j)].bitcast(FP8X4),
                         lhsT_scale=planes[w][4 * g : P, n0 : n0 + P],
                         rhs=codes[:, batch_cols].bitcast(FP8X4),
                         rhs_scale=plane[:, batch_cols],

@@ -23,9 +23,8 @@ TILES = HALF // P
 QUADS = 4
 LIVE = 16
 STORE_TILES = 2
+CUT_GROUPS = 2
 LAST_CUTS = 2
-LAST_PIECES = (2, 1, 1)
-SINGLE_STORES = 2
 
 FLOPS = 2 * 4 * HIDDEN * K * BATCH
 
@@ -59,16 +58,13 @@ def tile_naivelstm_pa_kernel(
         chunk_list = []
         for w in gate_weights[gate]:
             is_last_weight = (half, gate) == phases[-1] and w == gate_weights[gate][-1]
-            cuts = LAST_CUTS if is_last_weight else 1
-            for cut in range(cuts):
-                for g in range(GROUPS):
-                    if is_last_weight and cut == cuts - 1 and g == GROUPS - 1:
-                        tile0 = TILES - sum(LAST_PIECES)
-                        for tiles in LAST_PIECES:
-                            chunk_list.append((w, g, tile0, tiles))
-                            tile0 += tiles
-                    else:
-                        chunk_list.append((w, g, cut * (TILES // cuts), TILES // cuts))
+            if is_last_weight:
+                chunk_list.extend((w, g, 0, TILES) for g in range(GROUPS - CUT_GROUPS))
+                for cut in range(LAST_CUTS):
+                    for g in range(GROUPS - CUT_GROUPS, GROUPS):
+                        chunk_list.append((w, g, cut * (TILES // LAST_CUTS), TILES // LAST_CUTS))
+            else:
+                chunk_list.extend((w, g, 0, TILES) for g in range(GROUPS))
         phase_chunks.append(chunk_list)
     loads = [(w, g, 0, HALVES * TILES) for w in gate_weights["i"] for g in range(GROUPS)]
     for (half, gate), chunk_list in zip(phases, phase_chunks):
@@ -204,10 +200,8 @@ def tile_naivelstm_pa_kernel(
                     in0=gate_i[:, tile_index, :],
                     in1=gate_g[:, tile_index, :],
                 )
-                single = tile_index >= HALVES * TILES - SINGLE_STORES
-                if single or (tile_index + 1) % STORE_TILES == 0:
-                    first = tile_index if single else tile_index + 1 - STORE_TILES
-                    done = slice(first, tile_index + 1)
+                if (tile_index + 1) % STORE_TILES == 0:
+                    done = slice(tile_index + 1 - STORE_TILES, tile_index + 1)
                     nc.sync.dma_start(out=out_tiles[:, done, :], in_=product[:, done, :])
 
         for (half, gate), chunk_list in zip(phases, phase_chunks):

@@ -13,6 +13,7 @@ ACT = mybir.ActivationFunctionType
 
 P = 128
 PACK = 4
+ROWS = 16
 K = 2048
 GROUPS = K // (P * PACK)
 HIDDEN = 2048
@@ -60,9 +61,12 @@ def tile_naivelstm_pa_kernel(
             is_last_weight = (half, gate) == phases[-1] and w == gate_weights[gate][-1]
             if is_last_weight:
                 chunk_list.extend((w, g, 0, TILES) for g in range(GROUPS - CUT_GROUPS))
-                for cut in range(LAST_CUTS):
+                cut_tiles = TILES // LAST_CUTS
+                for tile0 in range(0, TILES, cut_tiles):
                     for g in range(GROUPS - CUT_GROUPS, GROUPS):
-                        chunk_list.append((w, g, cut * (TILES // LAST_CUTS), TILES // LAST_CUTS))
+                        chunk_list.append((w, g, tile0, cut_tiles))
+                w, g, tile0, tiles = chunk_list.pop()
+                chunk_list.extend((w, g, tile0 + half_piece, tiles // 2) for half_piece in (0, tiles // 2))
             else:
                 chunk_list.extend((w, g, 0, TILES) for g in range(GROUPS))
         phase_chunks.append(chunk_list)
@@ -75,7 +79,7 @@ def tile_naivelstm_pa_kernel(
         ctx.enter_context(tc.manual_schedule())
         keep = ctx.enter_context(tc.tile_pool(name="keep", bufs=1))
 
-        x_rows = keep.tile([P, GROUPS, PACK * BATCH], BF16)
+        x_rows = keep.tile([P, ROWS * BATCH], BF16)
         h_rows = keep.tile([P, K], BF16)
         bias_rows = keep.tile([P, P], BF16)
         planes = {}
@@ -100,9 +104,7 @@ def tile_naivelstm_pa_kernel(
         ident_bf16 = keep.tile([P, P], BF16)
         make_identity(nc, ident_bf16[:])
 
-        nc.sync.dma_start(
-            out=x_rows[:], in_=x.rearrange("(g p t) b -> p g (t b)", p=P, t=PACK)
-        )
+        nc.sync.dma_start(out=x_rows[:], in_=x.rearrange("(p c) b -> p (c b)", c=ROWS))
         nc.sync.dma_start(out=h_rows[:], in_=h)
         for i, b in enumerate((b_ii, b_hi, b_ig, b_hg)):
             rows = HIDDEN // P
@@ -124,11 +126,11 @@ def tile_naivelstm_pa_kernel(
             )
 
         x_grouped = keep.tile([P, GROUPS, BATCH, PACK], BF16, align_bytes=64)
-        nc.vector.tensor_copy(
-            out=x_grouped[:], in_=x_rows[:].rearrange("p g (t b) -> p g b t", t=PACK)
-        )
         x_codes = keep.tile([P, GROUPS * BATCH], U32, align_bytes=64)
         x_plane = keep.tile([P, GROUPS * BATCH], U8, align_bytes=64)
+        spread = keep.tile([P, PACK * P + PACK], BF16)
+        nc.vector.memset(spread[:], 0.0)
+        nc.vector.tensor_copy(out=spread[:, PACK - 1 : PACK * P + PACK - 1 : PACK], in_=ident_bf16[:])
 
         h_grouped = keep.tile([P, GROUPS, BATCH, PACK], BF16, align_bytes=64)
         h_codes = keep.tile([P, GROUPS * BATCH], U32, align_bytes=64)
@@ -136,6 +138,19 @@ def tile_naivelstm_pa_kernel(
         bias_f32 = keep.tile([P, 2, 2, HIDDEN // P], F32)
         bias_sum = keep.tile([P, 2, HIDDEN // P], F32)
         with tc.psum_pool(name="turn", bufs=1) as turn:
+            for g in range(GROUPS):
+                moved = turn.tile([P, PACK * BATCH], F32, name="moved_%d" % g)
+                for u in range(PACK):
+                    first = PACK - 1 + P * g - u
+                    nc.tensor.matmul(
+                        moved[:],
+                        lhsT=spread[:, first : first + P],
+                        rhs=x_rows[:, PACK * BATCH * u : PACK * BATCH * (u + 1)],
+                        start=u == 0,
+                        stop=u == PACK - 1,
+                    )
+                copy = nc.vector.tensor_copy if g % 2 == 0 else nc.scalar.copy
+                copy(out=x_grouped[:, g, :, :], in_=moved[:].rearrange("p (t b) -> p b t", t=PACK))
             h_words = h_rows[:].bitcast(F32)
             h_grouped_words = (
                 h_grouped[:]
@@ -208,7 +223,10 @@ def tile_naivelstm_pa_kernel(
             sums = []
             for j in range(TILES):
                 sums.append(psum.tile([P, BATCH], F32, name="sum_%d" % j, tag="sum_%d" % j))
-            for w, g, tile0, tiles in chunk_list:
+            pieces = chunk_list
+            if (half, gate) == (1, "i"):
+                pieces = [(w, g, j, 1) for j in range(TILES) for w, g, zero, all_tiles in chunk_list]
+            for w, g, tile0, tiles in pieces:
                 codes, plane = moving[w]
                 opens = w == gate_weights[gate][0] and g == 0
                 closes = w == gate_weights[gate][1] and g == GROUPS - 1

from contextlib import ExitStack

import concourse.mybir as mybir
from concourse.masks import make_identity

F32 = mybir.dt.float32
BF16 = mybir.dt.bfloat16
I32 = mybir.dt.int32
U32 = mybir.dt.uint32
U8 = mybir.dt.uint8
FP8X4 = mybir.dt.float8_e4m3fn_x4
ACT = mybir.ActivationFunctionType

P = 128
PACK = 4
ROWS = 16
K = 2048
GROUPS = K // (P * PACK)
HIDDEN = 2048
BATCH = 128
HALVES = 2
HALF = HIDDEN // HALVES
TILES = HALF // P
QUADS = 4
LIVE = 16
STORE_TILES = 2
CUT_GROUPS = 2
LAST_CUTS = 2

FLOPS = 2 * 4 * HIDDEN * K * BATCH


def tile_naivelstm_pa_kernel(
    tc,
    x,
    h,
    w_ii_words,
    w_ii_scales,
    w_ig_words,
    w_ig_scales,
    w_hi_words,
    w_hi_scales,
    w_hg_words,
    w_hg_scales,
    b_ii,
    b_hi,
    b_ig,
    b_hg,
    out,
):
    nc = tc.nc
    words = {"ii": w_ii_words, "hi": w_hi_words, "ig": w_ig_words, "hg": w_hg_words}
    scales = {"ii": w_ii_scales, "hi": w_hi_scales, "ig": w_ig_scales, "hg": w_hg_scales}
    gate_weights = {"i": ("ii", "hi"), "g": ("ig", "hg")}
    gate_column = {"i": 0, "g": 1}
    phases = [(half, gate) for gate in ("i", "g") for half in range(HALVES)]
    phase_chunks = []
    for half, gate in phases:
        chunk_list = []
        for w in gate_weights[gate]:
            is_last_weight = (half, gate) == phases[-1] and w == gate_weights[gate][-1]
            if is_last_weight:
                chunk_list.extend((w, g, 0, TILES) for g in range(GROUPS - CUT_GROUPS))
                cut_tiles = TILES // LAST_CUTS
                for tile0 in range(0, TILES, cut_tiles):
                    for g in range(GROUPS - CUT_GROUPS, GROUPS):
                        chunk_list.append((w, g, tile0, cut_tiles))
                w, g, tile0, tiles = chunk_list.pop()
                chunk_list.extend((w, g, tile0 + half_piece, tiles // 2) for half_piece in (0, tiles // 2))
            else:
                chunk_list.extend((w, g, 0, TILES) for g in range(GROUPS))
        phase_chunks.append(chunk_list)
    loads = [(w, g, 0, HALVES * TILES) for w in gate_weights["i"] for g in range(GROUPS)]
    for (half, gate), chunk_list in zip(phases, phase_chunks):
        if gate == "g":
            loads.extend((w, g, TILES * half + tile0, tiles) for w, g, tile0, tiles in chunk_list)

    with ExitStack() as ctx:
        ctx.enter_context(tc.manual_schedule())
        keep = ctx.enter_context(tc.tile_pool(name="keep", bufs=1))

        x_rows = keep.tile([P, ROWS * BATCH], BF16)
        h_rows = keep.tile([P, K], BF16)
        bias_rows = keep.tile([P, P], BF16)
        planes = {}
        for w in ("ii", "hi", "ig", "hg"):
            planes[w] = keep.tile([P, HIDDEN], U8, name="planes_" + w, align_bytes=64)
        load_tiles = []
        words_of = {}
        for w, g, first, tiles in loads:
            load_tile = keep.tile(
                [P, P * tiles], U32, name="words_%s_%d_%d" % (w, g, first), align_bytes=64
            )
            load_tiles.append(load_tile)
            for j in range(tiles):
                words_of[(w, g, first + j)] = load_tile[:, P * j : P * (j + 1)]

        for w in ("ii", "hi", "ig", "hg"):
            nc.vector.memset(planes[w][:].bitcast(I32), 0)
        nc.vector.memset(bias_rows[:], 0.0)

        ident_f32 = keep.tile([P, P], F32)
        make_identity(nc, ident_f32[:])
        ident_bf16 = keep.tile([P, P], BF16)
        make_identity(nc, ident_bf16[:])

        nc.sync.dma_start(out=x_rows[:], in_=x.rearrange("(p c) b -> p (c b)", c=ROWS))
        nc.sync.dma_start(out=h_rows[:], in_=h)
        for i, b in enumerate((b_ii, b_hi, b_ig, b_hg)):
            rows = HIDDEN // P
            nc.scalar.dma_start(
                out=bias_rows[rows * i : rows * (i + 1), :],
                in_=b.rearrange("(j p) o -> j (p o)", p=P),
            )
        for w in ("ii", "hi", "ig", "hg"):
            for quad in range(QUADS):
                nc.gpsimd.dma_start(
                    out=planes[w][32 * quad : 32 * quad + LIVE, :].bitcast(F32),
                    in_=scales[w][:, 4 * quad : 4 * quad + 4, :].bitcast(F32),
                )
        for (w, g, first, tiles), load_tile in zip(loads, load_tiles):
            load_bytes = slice(PACK * P * first, PACK * P * (first + tiles))
            nc.sync.dma_start(
                out=load_tile[:].bitcast(I32),
                in_=words[w][g].rearrange("p n t -> p (n t)")[:, load_bytes].bitcast(I32),
            )

        x_grouped = keep.tile([P, GROUPS, BATCH, PACK], BF16, align_bytes=64)
        x_codes = keep.tile([P, GROUPS * BATCH], U32, align_bytes=64)
        x_plane = keep.tile([P, GROUPS * BATCH], U8, align_bytes=64)
        spread = keep.tile([P, PACK * P + PACK], BF16)
        nc.vector.memset(spread[:], 0.0)
        nc.vector.tensor_copy(out=spread[:, PACK - 1 : PACK * P + PACK - 1 : PACK], in_=ident_bf16[:])

        h_grouped = keep.tile([P, GROUPS, BATCH, PACK], BF16, align_bytes=64)
        h_codes = keep.tile([P, GROUPS * BATCH], U32, align_bytes=64)
        h_plane = keep.tile([P, GROUPS * BATCH], U8, align_bytes=64)
        bias_f32 = keep.tile([P, 2, 2, HIDDEN // P], F32)
        bias_sum = keep.tile([P, 2, HIDDEN // P], F32)
        with tc.psum_pool(name="turn", bufs=1) as turn:
            for g in range(GROUPS):
                moved = turn.tile([P, PACK * BATCH], F32, name="moved_%d" % g)
                for u in range(PACK):
                    first = PACK - 1 + P * g - u
                    nc.tensor.matmul(
                        moved[:],
                        lhsT=spread[:, first : first + P],
                        rhs=x_rows[:, PACK * BATCH * u : PACK * BATCH * (u + 1)],
                        start=u == 0,
                        stop=u == PACK - 1,
                    )
                copy = nc.vector.tensor_copy if g % 2 == 0 else nc.scalar.copy
                copy(out=x_grouped[:, g, :, :], in_=moved[:].rearrange("p (t b) -> p b t", t=PACK))
            h_words = h_rows[:].bitcast(F32)
            h_grouped_words = (
                h_grouped[:]
                .rearrange("p g b t -> p (g b t)")
                .bitcast(F32)
                .rearrange("p (g b u) -> p g b u", g=GROUPS, u=2)
            )
            for pair in range(GROUPS // 2):
                turned = turn.tile([P, 2, 2, BATCH], F32, name="turned_%d" % pair)
                for gg in range(2):
                    g = 2 * pair + gg
                    for u in range(2):
                        nc.tensor.transpose(
                            turned[:, gg, u, :],
                            h_words[:, 256 * g + u : 256 * (g + 1) : 2],
                            ident_f32[:],
                        )
                nc.vector.tensor_copy(
                    out=h_grouped_words[:, 2 * pair : 2 * pair + 2, :, :],
                    in_=turned[:].rearrange("p g u b -> p g b u"),
                )
            nc.vector.quantize_mx(
                out=x_codes[:].bitcast(FP8X4),
                scales=x_plane[:],
                in_=x_grouped[:].rearrange("p g b t -> p (g b t)"),
            )
            nc.vector.quantize_mx(
                out=h_codes[:].bitcast(FP8X4),
                scales=h_plane[:],
                in_=h_grouped[:].rearrange("p g b t -> p (g b t)"),
            )
            bias_cols = turn.tile([P, P], BF16)
            nc.tensor.transpose(bias_cols[:], bias_rows[:], ident_bf16[:])
            nc.vector.tensor_copy(
                out=bias_f32[:].rearrange("p a s j -> p (a s j)"), in_=bias_cols[:, 0 : P // 2]
            )
            nc.vector.tensor_add(
                out=bias_sum[:], in0=bias_f32[:, :, 0, :], in1=bias_f32[:, :, 1, :]
            )
        moving = {"ii": (x_codes, x_plane), "ig": (x_codes, x_plane)}
        moving["hi"] = (h_codes, h_plane)
        moving["hg"] = (h_codes, h_plane)

        psum = ctx.enter_context(tc.psum_pool(name="psum", bufs=1))
        gate_i = keep.tile([P, HALVES * TILES, BATCH], F32)
        gate_g = keep.tile([P, HALVES * TILES, BATCH], F32)
        product = keep.tile([P, HALVES * TILES, BATCH], F32)
        out_tiles = out.rearrange("(j p) b -> p j b", p=P)

        def finish_tile(gate, tile_index, tile_sum):
            bias = bias_sum[:, gate_column[gate], tile_index : tile_index + 1]
            if gate == "i":
                nc.scalar.activation(
                    out=gate_i[:, tile_index, :], in_=tile_sum[:], func=ACT.Sigmoid, bias=bias
                )
            else:
                nc.scalar.activation(
                    out=gate_g[:, tile_index, :], in_=tile_sum[:], func=ACT.Tanh, bias=bias
                )
                nc.vector.tensor_mul(
                    out=product[:, tile_index, :],
                    in0=gate_i[:, tile_index, :],
                    in1=gate_g[:, tile_index, :],
                )
                if (tile_index + 1) % STORE_TILES == 0:
                    done = slice(tile_index + 1 - STORE_TILES, tile_index + 1)
                    nc.sync.dma_start(out=out_tiles[:, done, :], in_=product[:, done, :])

        for (half, gate), chunk_list in zip(phases, phase_chunks):
            sums = []
            for j in range(TILES):
                sums.append(psum.tile([P, BATCH], F32, name="sum_%d" % j, tag="sum_%d" % j))
            pieces = chunk_list
            if (half, gate) == (1, "i"):
                pieces = [(w, g, j, 1) for j in range(TILES) for w, g, zero, all_tiles in chunk_list]
            for w, g, tile0, tiles in pieces:
                codes, plane = moving[w]
                opens = w == gate_weights[gate][0] and g == 0
                closes = w == gate_weights[gate][1] and g == GROUPS - 1
                batch_cols = slice(BATCH * g, BATCH * (g + 1))
                for j in range(tile0, tile0 + tiles):
                    n0 = HALF * half + P * j
                    nc.tensor.matmul_mx(
                        out=sums[j][:],
                        lhsT=words_of[(w, g, TILES * half + j)].bitcast(FP8X4),
                        lhsT_scale=planes[w][4 * g : P, n0 : n0 + P],
                        rhs=codes[:, batch_cols].bitcast(FP8X4),
                        rhs_scale=plane[:, batch_cols],
                        start=opens,
                        stop=closes,
                    )
                if closes:
                    for j in range(tile0, tile0 + tiles):
                        finish_tile(gate, TILES * half + j, sums[j])
